import numpy as np
import ml_dtypes


def mxq(x, axis, fmt="e4m3"):
    dtype, down = {"e4m3": (ml_dtypes.float8_e4m3fn, 7), "e5m2": (ml_dtypes.float8_e5m2, 14)}[fmt]
    v = np.moveaxis(np.asarray(x, np.float32).astype(ml_dtypes.bfloat16).astype(np.float64), axis, -1)
    blocks = v.reshape(v.shape[:-1] + (-1, 32))
    amax = np.abs(blocks).max(-1, keepdims=True)
    byte = np.maximum(np.where(amax > 0, np.frexp(amax)[1] - 1 + 127, 0) - down, 1)
    scale = np.exp2(byte - 127.0)
    codes = (blocks / scale).astype(np.float32).astype(dtype).astype(np.float64)
    return np.moveaxis((codes * scale).reshape(v.shape), -1, axis)


WIDE = False


def mx_kscale(k):
    if not WIDE:
        return np.ones(k)
    levels = np.array([10, -10, 5, -5, 0])
    a = np.random.permutation(np.resize(levels, k // 512 * 4)).reshape(k // 512, 4)
    idx = np.arange(k)
    return np.exp2(a[idx // 512, idx % 128 // 32])


BF16 = ml_dtypes.bfloat16


def bf(x):
    return np.asarray(x, np.float32).astype(BF16)


def f64(x):
    return np.asarray(x).astype(np.float64)


N, DIN, DOUT, E, K, B = 1024, 8, 64, 16, 3, 16
C = DIN + DOUT
ES = 2.8 / np.sqrt(E)


def sigmoid(v):
    return 1.0 / (1.0 + np.exp(-v))


def draw_adj():
    g = np.random.standard_normal((N, N))
    l = ES**2 * np.sqrt(E) * (g + g.T) / np.sqrt(2.0)
    idx = np.arange(N)
    l[idx, idx] = ES**2 * (E + np.sqrt(2.0 * E) * np.random.standard_normal(N))
    l = np.maximum(l, 0.0)
    e = np.exp(l - l.max(1, keepdims=True))
    return e / e.sum(1, keepdims=True)


def setup_inputs():
    s = mx_kscale(N)
    adj = draw_adj()
    cheb2 = 2.0 * draw_adj() - np.eye(N)
    return {"adj": bf(adj * s[None, :]),
            "cheb2": bf(cheb2 * s[None, :]),
            "x": bf(np.random.standard_normal((B, N, DIN)) / s[None, :, None]),
            "state": bf(np.random.standard_normal((B, N, DOUT)) / s[None, :, None]),
            "r_logit": bf(np.random.standard_normal((B, N, DOUT)) * 0.8)}


def reference(adj, cheb2, x, state, r_logit):
    r = sigmoid(f64(r_logit))
    cand = np.concatenate([f64(x), r * f64(state)], axis=-1)
    cq = mxq(cand, 1, "e4m3")
    agg1 = mxq(f64(adj), 1, "e4m3") @ cq
    agg2 = mxq(f64(cheb2), 1, "e4m3") @ cq
    return np.stack([agg1, agg2], axis=2)

@@ -1,0 +1,189 @@
+import concourse.mybir as mybir
+from concourse.masks import make_identity
+
+F32 = mybir.dt.float32
+BF16 = mybir.dt.bfloat16
+U32 = mybir.dt.uint32
+U8 = mybir.dt.uint8
+FP8X4 = mybir.dt.float8_e4m3fn_x4
+
+P = 128
+PACK = 4
+PAIRS = PACK // 2
+K_PASS = P * PACK
+
+NODES = 1024
+BATCH = 16
+D_IN = 8
+D_STATE = 64
+D_CAND = D_IN + D_STATE
+MATS = 2
+
+PASSES = NODES // K_PASS
+ROW_TILES = NODES // P
+LOAD_TILES = 2
+X_COLS = BATCH * D_IN
+CHUNK_B = 4
+CHUNKS = BATCH // CHUNK_B
+CHUNK_COLS = CHUNK_B * D_STATE
+BANK_F32 = 512
+X_GROUPS = BANK_F32 // X_COLS
+
+FLOPS = 2 * MATS * NODES * NODES * BATCH * D_CAND
+
+
+def tile_agcrnlayer_pb_kernel(tc, adj, cheb2, x, state, r_logit, out):
+    nc = tc.nc
+
+    with tc.tile_pool(name="keep", bufs=1) as keep, tc.tile_pool(
+        name="stage", bufs=3
+    ) as stage, tc.psum_pool(name="psum", bufs=8) as psum:
+        ident = keep.tile([P, P], F32)
+        mat_sb = [
+            keep.tile([P, ROW_TILES, NODES], BF16, name="mat_sb%d" % s) for s in range(MATS)
+        ]
+        a_codes = keep.tile([P, MATS, ROW_TILES, PASSES, P], U32, align_bytes=64)
+        a_scales = keep.tile([P, MATS, ROW_TILES, PASSES, P], U8, align_bytes=64)
+
+        x_raw = keep.tile([P, PASSES, BATCH, PACK * D_IN], BF16)
+        x_grouped = keep.tile([P, PASSES, BATCH, D_IN, PACK], BF16, align_bytes=64)
+        x_codes = keep.tile([P, PASSES, X_COLS], U32, align_bytes=64)
+        x_scales = keep.tile([P, PASSES, X_COLS], U8, align_bytes=64)
+
+        raw_shape = [P, PASSES, CHUNK_B, PACK * D_STATE]
+        logit_raw = [keep.tile(raw_shape, BF16, name="logit_raw%d" % q) for q in range(CHUNKS)]
+        state_raw = [keep.tile(raw_shape, BF16, name="state_raw%d" % q) for q in range(CHUNKS)]
+        c_codes = [
+            keep.tile([P, PASSES, CHUNK_COLS], U32, name="c_codes%d" % q, align_bytes=64)
+            for q in range(CHUNKS)
+        ]
+        c_scales = [
+            keep.tile([P, PASSES, CHUNK_COLS], U8, name="c_scales%d" % q, align_bytes=64)
+            for q in range(CHUNKS)
+        ]
+        out_sb = [
+            keep.tile([P, CHUNK_B, ROW_TILES * MATS, D_CAND], F32, name="out_sb%d" % q)
+            for q in range(CHUNKS)
+        ]
+
+        def load_pass(queue, dst, src, g):
+            rows = src[:, g * K_PASS : (g + 1) * K_PASS, :]
+            queue.dma_start(out=dst, in_=rows.rearrange("b (p t) c -> p b (t c)", t=PACK))
+
+        def words_side_by_side(raw):
+            return raw.rearrange("p b (t c) -> p b c t", t=PACK)
+
+        def copy_out(index):
+            return nc.scalar.copy if index % 2 == 0 else nc.vector.tensor_copy
+
+        def multiply(acc, s, j, codes, scales):
+            for g in range(PASSES):
+                nc.tensor.matmul_mx(
+                    out=acc,
+                    lhsT=a_codes[:, s, j, g, :].bitcast(FP8X4),
+                    lhsT_scale=a_scales[:, s, j, g, :],
+                    rhs=codes[:, g, :].bitcast(FP8X4),
+                    rhs_scale=scales[:, g, :],
+                    start=(g == 0),
+                    stop=(g == PASSES - 1),
+                )
+
+        for g in range(PASSES):
+            load_pass(nc.scalar, x_raw[:, g], x, g)
+        for s, mat in enumerate((adj, cheb2)):
+            rows = mat.rearrange("(p j) n -> p j n", j=ROW_TILES)
+            for j in range(0, ROW_TILES, LOAD_TILES):
+                nc.sync.dma_start(
+                    out=mat_sb[s][:, j : j + LOAD_TILES, :], in_=rows[:, j : j + LOAD_TILES, :]
+                )
+        for q in range(CHUNKS):
+            batches = slice(q * CHUNK_B, (q + 1) * CHUNK_B)
+            for g in range(PASSES):
+                load_pass(nc.sync, logit_raw[q][:, g], r_logit[batches], g)
+                load_pass(nc.sync, state_raw[q][:, g], state[batches], g)
+
+        make_identity(nc, ident[:])
+
+        for g in range(PASSES):
+            nc.vector.tensor_copy(out=x_grouped[:, g], in_=words_side_by_side(x_raw[:, g]))
+        nc.vector.quantize_mx(
+            out=x_codes[:].rearrange("p g w -> p (g w)").bitcast(FP8X4),
+            scales=x_scales[:].rearrange("p g w -> p (g w)"),
+            in_=x_grouped[:].rearrange("p g b c t -> p (g b c t)"),
+        )
+
+        for s in range(MATS):
+            words = mat_sb[s][:].bitcast(F32)
+            for j in range(ROW_TILES):
+                flipped = psum.tile([P, PASSES, PAIRS, P], F32, tag="bank")
+                for g in range(PASSES):
+                    for u in range(PAIRS):
+                        first = g * P * PAIRS + u
+                        nc.tensor.transpose(
+                            flipped[:, g, u, :],
+                            words[:, j, first : (g + 1) * P * PAIRS : PAIRS],
+                            ident[:],
+                        )
+                grouped = stage.tile([P, PASSES, P, PACK], BF16, align_bytes=64)
+                copy_out(j)(
+                    out=grouped[:].bitcast(F32), in_=flipped[:].rearrange("p g u m -> p g m u")
+                )
+                nc.vector.quantize_mx(
+                    out=a_codes[:, s, j].rearrange("p g m -> p (g m)").bitcast(FP8X4),
+                    scales=a_scales[:, s, j].rearrange("p g m -> p (g m)"),
+                    in_=grouped[:].rearrange("p g m t -> p (g m t)"),
+                )
+
+        for first_row in range(0, ROW_TILES * MATS, X_GROUPS):
+            acc = psum.tile([P, X_GROUPS, X_COLS], F32, tag="bank")
+            for i in range(X_GROUPS):
+                row = first_row + i
+                multiply(acc[:, i, :], row % MATS, row // MATS, x_codes, x_scales)
+            for q in range(CHUNKS):
+                copy_out(first_row // X_GROUPS)(
+                    out=out_sb[q][:, :, first_row : first_row + X_GROUPS, 0:D_IN].rearrange(
+                        "p b r c -> p r b c"
+                    ),
+                    in_=acc[:, :, q * CHUNK_B * D_IN : (q + 1) * CHUNK_B * D_IN].rearrange(
+                        "p r (b c) -> p r b c", c=D_IN
+                    ),
+                )
+
+        for q in range(CHUNKS):
+            gate = stage.tile([P, PASSES, CHUNK_B, D_STATE, PACK], F32)
+            cand = stage.tile([P, PASSES, CHUNK_B, D_STATE, PACK], BF16, align_bytes=64)
+            for g in range(PASSES):
+                nc.scalar.activation(
+                    out=gate[:, g],
+                    in_=words_side_by_side(logit_raw[q][:, g]),
+                    func=mybir.ActivationFunctionType.Sigmoid,
+                )
+                nc.vector.tensor_tensor(
+                    out=cand[:, g],
+                    in0=gate[:, g],
+                    in1=words_side_by_side(state_raw[q][:, g]),
+                    op=mybir.AluOpType.mult,
+                )
+            nc.vector.quantize_mx(
+                out=c_codes[q][:].rearrange("p g w -> p (g w)").bitcast(FP8X4),
+                scales=c_scales[q][:].rearrange("p g w -> p (g w)"),
+                in_=cand[:].rearrange("p g b c t -> p (g b c t)"),
+            )
+
+            for j in range(ROW_TILES):
+                acc = psum.tile([P, MATS, CHUNK_COLS], F32, tag="bank")
+                for s in range(MATS):
+                    multiply(acc[:, s, :], s, j, c_codes[q], c_scales[q])
+                copy_out(j)(
+                    out=out_sb[q][:, :, j * MATS : (j + 1) * MATS, D_IN:D_CAND].rearrange(
+                        "p b s c -> p s b c"
+                    ),
+                    in_=acc[:].rearrange("p s (b c) -> p s b c", c=D_STATE),
+                )
+
+            nc.sync.dma_start(
+                out=out[q * CHUNK_B : (q + 1) * CHUNK_B].rearrange(
+                    "b (p j) s c -> p b (j s c)", j=ROW_TILES
+                ),
+                in_=out_sb[q][:].rearrange("p b r c -> p b (r c)"),
+            )

@@ -22,12 +22,16 @@ MATS = 2
 PASSES = NODES // K_PASS
 ROW_TILES = NODES // P
 LOAD_TILES = 2
+HALVES = 2
+HALF_TILES = ROW_TILES // HALVES
+HALF_ROWS = HALF_TILES * MATS
 X_COLS = BATCH * D_IN
 CHUNK_B = 4
 CHUNKS = BATCH // CHUNK_B
 CHUNK_COLS = CHUNK_B * D_STATE
 BANK_F32 = 512
 X_GROUPS = BANK_F32 // X_COLS
+PSUM_BANKS = 8
 
 FLOPS = 2 * MATS * NODES * NODES * BATCH * D_CAND
 
@@ -36,8 +40,10 @@ def tile_agcrnlayer_pb_kernel(tc, adj, cheb2, x, state, r_logit, out):
     nc = tc.nc
 
     with tc.tile_pool(name="keep", bufs=1) as keep, tc.tile_pool(
-        name="stage", bufs=3
-    ) as stage, tc.psum_pool(name="psum", bufs=8) as psum:
+        name="stage", bufs=2
+    ) as stage, tc.tile_pool(name="flip", bufs=4) as flip, tc.psum_pool(
+        name="psum", bufs=PSUM_BANKS
+    ) as psum, tc.manual_schedule():
         ident = keep.tile([P, P], F32)
         mat_sb = [
             keep.tile([P, ROW_TILES, NODES], BF16, name="mat_sb%d" % s) for s in range(MATS)
@@ -62,94 +68,27 @@ def tile_agcrnlayer_pb_kernel(tc, adj, cheb2, x, state, r_logit, out):
             for q in range(CHUNKS)
         ]
         out_sb = [
-            keep.tile([P, CHUNK_B, ROW_TILES * MATS, D_CAND], F32, name="out_sb%d" % q)
+            [
+                keep.tile([P, CHUNK_B, HALF_ROWS, D_CAND], F32, name="out_sb%d_%d" % (q, h))
+                for h in range(HALVES)
+            ]
             for q in range(CHUNKS)
         ]
 
-        def load_pass(queue, dst, src, g):
-            rows = src[:, g * K_PASS : (g + 1) * K_PASS, :]
-            queue.dma_start(out=dst, in_=rows.rearrange("b (p t) c -> p b (t c)", t=PACK))
+        def load_pass(dst, src, g):
+            k_rows = src[:, g * K_PASS : (g + 1) * K_PASS, :]
+            nc.sync.dma_start(out=dst, in_=k_rows.rearrange("b (p t) c -> p b (t c)", t=PACK))
+
+        def load_chunk(q):
+            batches = slice(q * CHUNK_B, (q + 1) * CHUNK_B)
+            for g in range(PASSES):
+                load_pass(logit_raw[q][:, g], r_logit[batches], g)
+                load_pass(state_raw[q][:, g], state[batches], g)
 
         def words_side_by_side(raw):
             return raw.rearrange("p b (t c) -> p b c t", t=PACK)
 
-        def copy_out(index):
-            return nc.scalar.copy if index % 2 == 0 else nc.vector.tensor_copy
-
-        def multiply(acc, s, j, codes, scales):
-            for g in range(PASSES):
-                nc.tensor.matmul_mx(
-                    out=acc,
-                    lhsT=a_codes[:, s, j, g, :].bitcast(FP8X4),
-                    lhsT_scale=a_scales[:, s, j, g, :],
-                    rhs=codes[:, g, :].bitcast(FP8X4),
-                    rhs_scale=scales[:, g, :],
-                    start=(g == 0),
-                    stop=(g == PASSES - 1),
-                )
-
-        for g in range(PASSES):
-            load_pass(nc.scalar, x_raw[:, g], x, g)
-        for s, mat in enumerate((adj, cheb2)):
-            rows = mat.rearrange("(p j) n -> p j n", j=ROW_TILES)
-            for j in range(0, ROW_TILES, LOAD_TILES):
-                nc.sync.dma_start(
-                    out=mat_sb[s][:, j : j + LOAD_TILES, :], in_=rows[:, j : j + LOAD_TILES, :]
-                )
-        for q in range(CHUNKS):
-            batches = slice(q * CHUNK_B, (q + 1) * CHUNK_B)
-            for g in range(PASSES):
-                load_pass(nc.sync, logit_raw[q][:, g], r_logit[batches], g)
-                load_pass(nc.sync, state_raw[q][:, g], state[batches], g)
-
-        make_identity(nc, ident[:])
-
-        for g in range(PASSES):
-            nc.vector.tensor_copy(out=x_grouped[:, g], in_=words_side_by_side(x_raw[:, g]))
-        nc.vector.quantize_mx(
-            out=x_codes[:].rearrange("p g w -> p (g w)").bitcast(FP8X4),
-            scales=x_scales[:].rearrange("p g w -> p (g w)"),
-            in_=x_grouped[:].rearrange("p g b c t -> p (g b c t)"),
-        )
-
-        for s in range(MATS):
-            words = mat_sb[s][:].bitcast(F32)
-            for j in range(ROW_TILES):
-                flipped = psum.tile([P, PASSES, PAIRS, P], F32, tag="bank")
-                for g in range(PASSES):
-                    for u in range(PAIRS):
-                        first = g * P * PAIRS + u
-                        nc.tensor.transpose(
-                            flipped[:, g, u, :],
-                            words[:, j, first : (g + 1) * P * PAIRS : PAIRS],
-                            ident[:],
-                        )
-                grouped = stage.tile([P, PASSES, P, PACK], BF16, align_bytes=64)
-                copy_out(j)(
-                    out=grouped[:].bitcast(F32), in_=flipped[:].rearrange("p g u m -> p g m u")
-                )
-                nc.vector.quantize_mx(
-                    out=a_codes[:, s, j].rearrange("p g m -> p (g m)").bitcast(FP8X4),
-                    scales=a_scales[:, s, j].rearrange("p g m -> p (g m)"),
-                    in_=grouped[:].rearrange("p g m t -> p (g m t)"),
-                )
-
-        for first_row in range(0, ROW_TILES * MATS, X_GROUPS):
-            acc = psum.tile([P, X_GROUPS, X_COLS], F32, tag="bank")
-            for i in range(X_GROUPS):
-                row = first_row + i
-                multiply(acc[:, i, :], row % MATS, row // MATS, x_codes, x_scales)
-            for q in range(CHUNKS):
-                copy_out(first_row // X_GROUPS)(
-                    out=out_sb[q][:, :, first_row : first_row + X_GROUPS, 0:D_IN].rearrange(
-                        "p b r c -> p r b c"
-                    ),
-                    in_=acc[:, :, q * CHUNK_B * D_IN : (q + 1) * CHUNK_B * D_IN].rearrange(
-                        "p r (b c) -> p r b c", c=D_IN
-                    ),
-                )
-
-        for q in range(CHUNKS):
+        def gate_chunk(q):
             gate = stage.tile([P, PASSES, CHUNK_B, D_STATE, PACK], F32)
             cand = stage.tile([P, PASSES, CHUNK_B, D_STATE, PACK], BF16, align_bytes=64)
             for g in range(PASSES):
@@ -170,20 +109,101 @@ def tile_agcrnlayer_pb_kernel(tc, adj, cheb2, x, state, r_logit, out):
                 in_=cand[:].rearrange("p g b c t -> p (g b c t)"),
             )
 
-            for j in range(ROW_TILES):
-                acc = psum.tile([P, MATS, CHUNK_COLS], F32, tag="bank")
-                for s in range(MATS):
-                    multiply(acc[:, s, :], s, j, c_codes[q], c_scales[q])
-                copy_out(j)(
-                    out=out_sb[q][:, :, j * MATS : (j + 1) * MATS, D_IN:D_CAND].rearrange(
-                        "p b s c -> p s b c"
-                    ),
-                    in_=acc[:].rearrange("p s (b c) -> p s b c", c=D_STATE),
+        def multiply(acc, s, j, codes, scales):
+            for g in range(PASSES):
+                nc.tensor.matmul_mx(
+                    out=acc,
+                    lhsT=a_codes[:, s, j, g, :].bitcast(FP8X4),
+                    lhsT_scale=a_scales[:, s, j, g, :],
+                    rhs=codes[:, g, :].bitcast(FP8X4),
+                    rhs_scale=scales[:, g, :],
+                    start=(g == 0),
+                    stop=(g == PASSES - 1),
                 )
 
-            nc.sync.dma_start(
-                out=out[q * CHUNK_B : (q + 1) * CHUNK_B].rearrange(
-                    "b (p j) s c -> p b (j s c)", j=ROW_TILES
-                ),
-                in_=out_sb[q][:].rearrange("p b r c -> p b (r c)"),
-            )
+        make_identity(nc, ident[:])
+
+        load_chunk(0)
+        for s, mat in enumerate((adj, cheb2)):
+            tiles = mat.rearrange("(p j) n -> p j n", j=ROW_TILES)
+            for j in range(0, ROW_TILES, LOAD_TILES):
+                nc.sync.dma_start(
+                    out=mat_sb[s][:, j : j + LOAD_TILES, :], in_=tiles[:, j : j + LOAD_TILES, :]
+                )
+        for g in range(PASSES):
+            load_pass(x_raw[:, g], x, g)
+        for q in range(1, CHUNKS):
+            load_chunk(q)
+
+        gate_chunk(0)
+
+        for s in range(MATS):
+            words = mat_sb[s][:].bitcast(F32)
+            for j in range(ROW_TILES):
+                flipped = psum.tile([P, PASSES, PAIRS, P], F32, tag="bank")
+                for g in range(PASSES):
+                    for u in range(PAIRS):
+                        first = g * P * PAIRS + u
+                        nc.tensor.transpose(
+                            flipped[:, g, u, :],
+                            words[:, j, first : (g + 1) * P * PAIRS : PAIRS],
+                            ident[:],
+                        )
+                grouped = flip.tile([P, PASSES, P, PACK], BF16, align_bytes=64)
+                nc.scalar.copy(
+                    out=grouped[:].bitcast(F32), in_=flipped[:].rearrange("p g u m -> p g m u")
+                )
+                nc.vector.quantize_mx(
+                    out=a_codes[:, s, j].rearrange("p g m -> p (g m)").bitcast(FP8X4),
+                    scales=a_scales[:, s, j].rearrange("p g m -> p (g m)"),
+                    in_=grouped[:].rearrange("p g m t -> p (g m t)"),
+                )
+
+        for g in range(PASSES):
+            nc.vector.tensor_copy(out=x_grouped[:, g], in_=words_side_by_side(x_raw[:, g]))
+        nc.vector.quantize_mx(
+            out=x_codes[:].rearrange("p g w -> p (g w)").bitcast(FP8X4),
+            scales=x_scales[:].rearrange("p g w -> p (g w)"),
+            in_=x_grouped[:].rearrange("p g b c t -> p (g b c t)"),
+        )
+
+        for h in range(HALVES):
+            for first_row in range(0, HALF_ROWS, X_GROUPS):
+                acc = psum.tile([P, X_GROUPS, X_COLS], F32, tag="bank")
+                for i in range(X_GROUPS):
+                    row = first_row + i
+                    multiply(
+                        acc[:, i, :], row % MATS, h * HALF_TILES + row // MATS, x_codes, x_scales
+                    )
+                even = (first_row // X_GROUPS) % 2 == 0
+                for q in range(CHUNKS):
+                    (nc.scalar.copy if even else nc.vector.tensor_copy)(
+                        out=out_sb[q][h][:, :, first_row : first_row + X_GROUPS, 0:D_IN].rearrange(
+                            "p b r c -> p r b c"
+                        ),
+                        in_=acc[:, :, q * CHUNK_B * D_IN : (q + 1) * CHUNK_B * D_IN].rearrange(
+                            "p r (b c) -> p r b c", c=D_IN
+                        ),
+                    )
+
+        for q in range(CHUNKS):
+            if q + 1 < CHUNKS:
+                gate_chunk(q + 1)
+            for h in range(HALVES):
+                empty_bank = nc.scalar.copy if h == 0 else nc.vector.tensor_copy
+                for i in range(HALF_TILES):
+                    acc = psum.tile([P, MATS, CHUNK_COLS], F32, tag="bank")
+                    for s in range(MATS):
+                        multiply(acc[:, s, :], s, h * HALF_TILES + i, c_codes[q], c_scales[q])
+                    empty_bank(
+                        out=out_sb[q][h][:, :, i * MATS : (i + 1) * MATS, D_IN:D_CAND].rearrange(
+                            "p b s c -> p s b c"
+                        ),
+                        in_=acc[:].rearrange("p s (b c) -> p s b c", c=D_STATE),
+                    )
+                nc.sync.dma_start(
+                    out=out[q * CHUNK_B : (q + 1) * CHUNK_B].rearrange(
+                        "b (p j) s c -> p b j (s c)", j=ROW_TILES
+                    )[:, :, h * HALF_TILES : (h + 1) * HALF_TILES, :],
+                    in_=out_sb[q][h][:].rearrange("p b (i s) c -> p b i (s c)", s=MATS),
+                )

@@ -68,12 +68,11 @@ def tile_agcrnlayer_pb_kernel(tc, adj, cheb2, x, state, r_logit, out):
             for q in range(CHUNKS)
         ]
         out_sb = [
-            [
-                keep.tile([P, CHUNK_B, HALF_ROWS, D_CAND], F32, name="out_sb%d_%d" % (q, h))
-                for h in range(HALVES)
-            ]
-            for q in range(CHUNKS)
+            keep.tile([P, BATCH, HALF_ROWS, D_CAND], F32, name="out_sb%d" % h)
+            for h in range(HALVES)
         ]
+        gates = {}
+        cands = {}
 
         def load_pass(dst, src, g):
             k_rows = src[:, g * K_PASS : (g + 1) * K_PASS, :]
@@ -85,29 +84,71 @@ def tile_agcrnlayer_pb_kernel(tc, adj, cheb2, x, state, r_logit, out):
                 load_pass(logit_raw[q][:, g], r_logit[batches], g)
                 load_pass(state_raw[q][:, g], state[batches], g)
 
+        def load_matrices(h):
+            for j in range(h * HALF_TILES, (h + 1) * HALF_TILES, LOAD_TILES):
+                for s, mat in enumerate((adj, cheb2)):
+                    tiles = mat.rearrange("(p j) n -> p j n", j=ROW_TILES)
+                    nc.sync.dma_start(
+                        out=mat_sb[s][:, j : j + LOAD_TILES, :],
+                        in_=tiles[:, j : j + LOAD_TILES, :],
+                    )
+
         def words_side_by_side(raw):
             return raw.rearrange("p b (t c) -> p b c t", t=PACK)
 
-        def gate_chunk(q):
-            gate = stage.tile([P, PASSES, CHUNK_B, D_STATE, PACK], F32)
-            cand = stage.tile([P, PASSES, CHUNK_B, D_STATE, PACK], BF16, align_bytes=64)
-            for g in range(PASSES):
-                nc.scalar.activation(
-                    out=gate[:, g],
-                    in_=words_side_by_side(logit_raw[q][:, g]),
-                    func=mybir.ActivationFunctionType.Sigmoid,
+        def gate_sigmoid(q, g):
+            if g == 0:
+                gates[q] = stage.tile([P, PASSES, CHUNK_B, D_STATE, PACK], F32, name="gate")
+                cands[q] = stage.tile(
+                    [P, PASSES, CHUNK_B, D_STATE, PACK], BF16, name="cand", align_bytes=64
                 )
-                nc.vector.tensor_tensor(
-                    out=cand[:, g],
-                    in0=gate[:, g],
-                    in1=words_side_by_side(state_raw[q][:, g]),
-                    op=mybir.AluOpType.mult,
-                )
+            nc.scalar.activation(
+                out=gates[q][:, g],
+                in_=words_side_by_side(logit_raw[q][:, g]),
+                func=mybir.ActivationFunctionType.Sigmoid,
+            )
+
+        def gate_product(q, g):
+            nc.vector.tensor_tensor(
+                out=cands[q][:, g],
+                in0=gates[q][:, g],
+                in1=words_side_by_side(state_raw[q][:, g]),
+                op=mybir.AluOpType.mult,
+            )
+
+        def gate_quantise(q):
             nc.vector.quantize_mx(
                 out=c_codes[q][:].rearrange("p g w -> p (g w)").bitcast(FP8X4),
                 scales=c_scales[q][:].rearrange("p g w -> p (g w)"),
-                in_=cand[:].rearrange("p g b c t -> p (g b c t)"),
+                in_=cands[q][:].rearrange("p g b c t -> p (g b c t)"),
             )
+
+        def transpose_tile(s, j):
+            words = mat_sb[s][:].bitcast(F32)
+            flipped = psum.tile([P, PASSES, PAIRS, P], F32, tag="bank")
+            for g in range(PASSES):
+                for u in range(PAIRS):
+                    first = g * P * PAIRS + u
+                    nc.tensor.transpose(
+                        flipped[:, g, u, :],
+                        words[:, j, first : (g + 1) * P * PAIRS : PAIRS],
+                        ident[:],
+                    )
+            grouped = flip.tile([P, PASSES, P, PACK], BF16, align_bytes=64)
+            nc.scalar.copy(
+                out=grouped[:].bitcast(F32), in_=flipped[:].rearrange("p g u m -> p g m u")
+            )
+            nc.vector.quantize_mx(
+                out=a_codes[:, s, j].rearrange("p g m -> p (g m)").bitcast(FP8X4),
+                scales=a_scales[:, s, j].rearrange("p g m -> p (g m)"),
+                in_=grouped[:].rearrange("p g m t -> p (g m t)"),
+            )
+
+        def transpose_half(h):
+            for j in range(h * HALF_TILES, (h + 1) * HALF_TILES, LOAD_TILES):
+                for s in range(MATS):
+                    for k in range(LOAD_TILES):
+                        transpose_tile(s, j + k)
 
         def multiply(acc, s, j, codes, scales):
             for g in range(PASSES):
@@ -121,43 +162,75 @@ def tile_agcrnlayer_pb_kernel(tc, adj, cheb2, x, state, r_logit, out):
                     stop=(g == PASSES - 1),
                 )
 
+        def empty_bank(turn):
+            return nc.scalar.copy if turn % 2 == 0 else nc.vector.tensor_copy
+
+        def chunk_bank(q, h, i):
+            acc = psum.tile([P, MATS, CHUNK_COLS], F32, tag="bank")
+            for s in range(MATS):
+                multiply(acc[:, s, :], s, h * HALF_TILES + i, c_codes[q], c_scales[q])
+            empty_bank(i)(
+                out=out_sb[h][
+                    :, q * CHUNK_B : (q + 1) * CHUNK_B, i * MATS : (i + 1) * MATS, D_IN:D_CAND
+                ].rearrange("p b s c -> p s b c"),
+                in_=acc[:].rearrange("p s (b c) -> p s b c", c=D_STATE),
+            )
+
+        def x_banks(h):
+            for first_row in range(0, HALF_ROWS, X_GROUPS):
+                acc = psum.tile([P, X_GROUPS, X_COLS], F32, tag="bank")
+                for i in range(X_GROUPS):
+                    row = first_row + i
+                    multiply(
+                        acc[:, i, :], row % MATS, h * HALF_TILES + row // MATS, x_codes, x_scales
+                    )
+                empty_bank(first_row // X_GROUPS)(
+                    out=out_sb[h][:, :, first_row : first_row + X_GROUPS, 0:D_IN].rearrange(
+                        "p b r c -> p r b c"
+                    ),
+                    in_=acc[:].rearrange("p r (b c) -> p r b c", c=D_IN),
+                )
+
+        def store(q, h):
+            batches = slice(q * CHUNK_B, (q + 1) * CHUNK_B)
+            nc.sync.dma_start(
+                out=out[batches].rearrange("b (p j) s c -> p b j (s c)", j=ROW_TILES)[
+                    :, :, h * HALF_TILES : (h + 1) * HALF_TILES, :
+                ],
+                in_=out_sb[h][:, batches].rearrange("p b (i s) c -> p b i (s c)", s=MATS),
+            )
+
+        def chunk_half(q, h, gate_next=None, with_x=False):
+            for i in range(HALF_TILES):
+                if gate_next is not None:
+                    if i % 2 == 0:
+                        gate_sigmoid(gate_next, i // 2)
+                    else:
+                        gate_product(gate_next, i // 2)
+                chunk_bank(q, h, i)
+            if gate_next is not None:
+                gate_quantise(gate_next)
+            if with_x:
+                x_banks(h)
+            store(q, h)
+
         make_identity(nc, ident[:])
 
         load_chunk(0)
-        for s, mat in enumerate((adj, cheb2)):
-            tiles = mat.rearrange("(p j) n -> p j n", j=ROW_TILES)
-            for j in range(0, ROW_TILES, LOAD_TILES):
-                nc.sync.dma_start(
-                    out=mat_sb[s][:, j : j + LOAD_TILES, :], in_=tiles[:, j : j + LOAD_TILES, :]
-                )
+        load_matrices(0)
         for g in range(PASSES):
             load_pass(x_raw[:, g], x, g)
-        for q in range(1, CHUNKS):
-            load_chunk(q)
+        load_chunk(1)
+        load_matrices(1)
+        load_chunk(2)
+        load_chunk(3)
 
-        gate_chunk(0)
+        for g in range(PASSES):
+            gate_sigmoid(0, g)
+            gate_product(0, g)
+        gate_quantise(0)
 
-        for s in range(MATS):
-            words = mat_sb[s][:].bitcast(F32)
-            for j in range(ROW_TILES):
-                flipped = psum.tile([P, PASSES, PAIRS, P], F32, tag="bank")
-                for g in range(PASSES):
-                    for u in range(PAIRS):
-                        first = g * P * PAIRS + u
-                        nc.tensor.transpose(
-                            flipped[:, g, u, :],
-                            words[:, j, first : (g + 1) * P * PAIRS : PAIRS],
-                            ident[:],
-                        )
-                grouped = flip.tile([P, PASSES, P, PACK], BF16, align_bytes=64)
-                nc.scalar.copy(
-                    out=grouped[:].bitcast(F32), in_=flipped[:].rearrange("p g u m -> p g m u")
-                )
-                nc.vector.quantize_mx(
-                    out=a_codes[:, s, j].rearrange("p g m -> p (g m)").bitcast(FP8X4),
-                    scales=a_scales[:, s, j].rearrange("p g m -> p (g m)"),
-                    in_=grouped[:].rearrange("p g m t -> p (g m t)"),
-                )
+        transpose_half(0)
 
         for g in range(PASSES):
             nc.vector.tensor_copy(out=x_grouped[:, g], in_=words_side_by_side(x_raw[:, g]))
@@ -167,43 +240,12 @@ def tile_agcrnlayer_pb_kernel(tc, adj, cheb2, x, state, r_logit, out):
             in_=x_grouped[:].rearrange("p g b c t -> p (g b c t)"),
         )
 
-        for h in range(HALVES):
-            for first_row in range(0, HALF_ROWS, X_GROUPS):
-                acc = psum.tile([P, X_GROUPS, X_COLS], F32, tag="bank")
-                for i in range(X_GROUPS):
-                    row = first_row + i
-                    multiply(
-                        acc[:, i, :], row % MATS, h * HALF_TILES + row // MATS, x_codes, x_scales
-                    )
-                even = (first_row // X_GROUPS) % 2 == 0
-                for q in range(CHUNKS):
-                    (nc.scalar.copy if even else nc.vector.tensor_copy)(
-                        out=out_sb[q][h][:, :, first_row : first_row + X_GROUPS, 0:D_IN].rearrange(
-                            "p b r c -> p r b c"
-                        ),
-                        in_=acc[:, :, q * CHUNK_B * D_IN : (q + 1) * CHUNK_B * D_IN].rearrange(
-                            "p r (b c) -> p r b c", c=D_IN
-                        ),
-                    )
-
-        for q in range(CHUNKS):
-            if q + 1 < CHUNKS:
-                gate_chunk(q + 1)
-            for h in range(HALVES):
-                empty_bank = nc.scalar.copy if h == 0 else nc.vector.tensor_copy
-                for i in range(HALF_TILES):
-                    acc = psum.tile([P, MATS, CHUNK_COLS], F32, tag="bank")
-                    for s in range(MATS):
-                        multiply(acc[:, s, :], s, h * HALF_TILES + i, c_codes[q], c_scales[q])
-                    empty_bank(
-                        out=out_sb[q][h][:, :, i * MATS : (i + 1) * MATS, D_IN:D_CAND].rearrange(
-                            "p b s c -> p s b c"
-                        ),
-                        in_=acc[:].rearrange("p s (b c) -> p s b c", c=D_STATE),
-                    )
-                nc.sync.dma_start(
-                    out=out[q * CHUNK_B : (q + 1) * CHUNK_B].rearrange(
-                        "b (p j) s c -> p b j (s c)", j=ROW_TILES
-                    )[:, :, h * HALF_TILES : (h + 1) * HALF_TILES, :],
-                    in_=out_sb[q][h][:].rearrange("p b (i s) c -> p b i (s c)", s=MATS),
-                )
+        chunk_half(0, 0, gate_next=1, with_x=True)
+        transpose_half(1)
+        chunk_half(1, 0, gate_next=2)
+        chunk_half(0, 1, with_x=True)
+        chunk_half(1, 1)
+        chunk_half(2, 0, gate_next=3)
+        chunk_half(2, 1)
+        chunk_half(3, 0)
+        chunk_half(3, 1)

@@ -73,6 +73,7 @@ def tile_agcrnlayer_pb_kernel(tc, adj, cheb2, x, state, r_logit, out):
         ]
         gates = {}
         cands = {}
+        waiting = []
 
         def load_pass(dst, src, g):
             k_rows = src[:, g * K_PASS : (g + 1) * K_PASS, :]
@@ -116,14 +117,23 @@ def tile_agcrnlayer_pb_kernel(tc, adj, cheb2, x, state, r_logit, out):
                 op=mybir.AluOpType.mult,
             )
 
-        def gate_quantise(q):
+        def gate_quantise(q, g):
             nc.vector.quantize_mx(
-                out=c_codes[q][:].rearrange("p g w -> p (g w)").bitcast(FP8X4),
-                scales=c_scales[q][:].rearrange("p g w -> p (g w)"),
-                in_=cands[q][:].rearrange("p g b c t -> p (g b c t)"),
+                out=c_codes[q][:, g, :].bitcast(FP8X4),
+                scales=c_scales[q][:, g, :],
+                in_=cands[q][:, g].rearrange("p b c t -> p (b c t)"),
             )
 
-        def transpose_tile(s, j):
+        def quantise_waiting():
+            s, j, grouped = waiting[0]
+            waiting.clear()
+            nc.vector.quantize_mx(
+                out=a_codes[:, s, j].rearrange("p g m -> p (g m)").bitcast(FP8X4),
+                scales=a_scales[:, s, j].rearrange("p g m -> p (g m)"),
+                in_=grouped[:].rearrange("p g m t -> p (g m t)"),
+            )
+
+        def transpose_tile(s, j, turn):
             words = mat_sb[s][:].bitcast(F32)
             flipped = psum.tile([P, PASSES, PAIRS, P], F32, tag="bank")
             for g in range(PASSES):
@@ -135,20 +145,21 @@ def tile_agcrnlayer_pb_kernel(tc, adj, cheb2, x, state, r_logit, out):
                         ident[:],
                     )
             grouped = flip.tile([P, PASSES, P, PACK], BF16, align_bytes=64)
-            nc.scalar.copy(
+            (nc.vector.tensor_copy if turn % 4 == 3 else nc.scalar.copy)(
                 out=grouped[:].bitcast(F32), in_=flipped[:].rearrange("p g u m -> p g m u")
             )
-            nc.vector.quantize_mx(
-                out=a_codes[:, s, j].rearrange("p g m -> p (g m)").bitcast(FP8X4),
-                scales=a_scales[:, s, j].rearrange("p g m -> p (g m)"),
-                in_=grouped[:].rearrange("p g m t -> p (g m t)"),
-            )
+            if waiting:
+                quantise_waiting()
+            waiting.append((s, j, grouped))
 
         def transpose_half(h):
+            turn = 0
             for j in range(h * HALF_TILES, (h + 1) * HALF_TILES, LOAD_TILES):
                 for s in range(MATS):
                     for k in range(LOAD_TILES):
-                        transpose_tile(s, j + k)
+                        transpose_tile(s, j + k, turn)
+                        turn += 1
+            quantise_waiting()
 
         def multiply(acc, s, j, codes, scales):
             for g in range(PASSES):
@@ -200,16 +211,16 @@ def tile_agcrnlayer_pb_kernel(tc, adj, cheb2, x, state, r_logit, out):
                 in_=out_sb[h][:, batches].rearrange("p b (i s) c -> p b i (s c)", s=MATS),
             )
 
-        def chunk_half(q, h, gate_next=None, with_x=False):
+        def chunk_half(q, h, gate=None, with_x=False):
             for i in range(HALF_TILES):
-                if gate_next is not None:
-                    if i % 2 == 0:
-                        gate_sigmoid(gate_next, i // 2)
-                    else:
-                        gate_product(gate_next, i // 2)
+                if gate is not None:
+                    if i == 0:
+                        gate_sigmoid(gate[0], gate[1])
+                    elif i == 1:
+                        gate_product(gate[0], gate[1])
+                    elif i == 3:
+                        gate_quantise(gate[0], gate[1])
                 chunk_bank(q, h, i)
-            if gate_next is not None:
-                gate_quantise(gate_next)
             if with_x:
                 x_banks(h)
             store(q, h)
@@ -218,9 +229,9 @@ def tile_agcrnlayer_pb_kernel(tc, adj, cheb2, x, state, r_logit, out):
 
         load_chunk(0)
         load_matrices(0)
+        load_chunk(1)
         for g in range(PASSES):
             load_pass(x_raw[:, g], x, g)
-        load_chunk(1)
         load_matrices(1)
         load_chunk(2)
         load_chunk(3)
@@ -228,10 +239,17 @@ def tile_agcrnlayer_pb_kernel(tc, adj, cheb2, x, state, r_logit, out):
         for g in range(PASSES):
             gate_sigmoid(0, g)
             gate_product(0, g)
-        gate_quantise(0)
+        for g in range(PASSES):
+            gate_quantise(0, g)
 
         transpose_half(0)
-
+        for g in range(PASSES):
+            gate_sigmoid(1, g)
+            gate_product(1, g)
+        for i in range(HALF_TILES):
+            chunk_bank(0, 0, i)
+        for g in range(PASSES):
+            gate_quantise(1, g)
         for g in range(PASSES):
             nc.vector.tensor_copy(out=x_grouped[:, g], in_=words_side_by_side(x_raw[:, g]))
         nc.vector.quantize_mx(
@@ -240,12 +258,13 @@ def tile_agcrnlayer_pb_kernel(tc, adj, cheb2, x, state, r_logit, out):
             in_=x_grouped[:].rearrange("p g b c t -> p (g b c t)"),
         )
 
-        chunk_half(0, 0, gate_next=1, with_x=True)
         transpose_half(1)
-        chunk_half(1, 0, gate_next=2)
-        chunk_half(0, 1, with_x=True)
-        chunk_half(1, 1)
-        chunk_half(2, 0, gate_next=3)
+        x_banks(0)
+        store(0, 0)
+        chunk_half(1, 0, gate=(2, 0))
+        chunk_half(0, 1, gate=(2, 1), with_x=True)
+        chunk_half(1, 1, gate=(3, 0))
+        chunk_half(2, 0, gate=(3, 1))
         chunk_half(2, 1)
         chunk_half(3, 0)
         chunk_half(3, 1)

@@ -99,20 +99,20 @@ def tile_agcrnlayer_pb_kernel(tc, adj, cheb2, x, state, r_logit, out):
 
         def gate_sigmoid(q, g):
             if g == 0:
-                gates[q] = stage.tile([P, PASSES, CHUNK_B, D_STATE, PACK], F32, name="gate")
+                gates[q] = stage.tile([P, PASSES, CHUNK_B, PACK, D_STATE], F32, name="gate")
                 cands[q] = stage.tile(
                     [P, PASSES, CHUNK_B, D_STATE, PACK], BF16, name="cand", align_bytes=64
                 )
             nc.scalar.activation(
-                out=gates[q][:, g],
-                in_=words_side_by_side(logit_raw[q][:, g]),
+                out=gates[q][:, g].rearrange("p b t c -> p b (t c)"),
+                in_=logit_raw[q][:, g],
                 func=mybir.ActivationFunctionType.Sigmoid,
             )
 
         def gate_product(q, g):
             nc.vector.tensor_tensor(
                 out=cands[q][:, g],
-                in0=gates[q][:, g],
+                in0=gates[q][:, g].rearrange("p b t c -> p b c t"),
                 in1=words_side_by_side(state_raw[q][:, g]),
                 op=mybir.AluOpType.mult,
             )

@@ -176,11 +176,11 @@ def tile_agcrnlayer_pb_kernel(tc, adj, cheb2, x, state, r_logit, out):
         def empty_bank(turn):
             return nc.scalar.copy if turn % 2 == 0 else nc.vector.tensor_copy
 
-        def chunk_bank(q, h, i):
+        def chunk_bank(q, h, i, turn):
             acc = psum.tile([P, MATS, CHUNK_COLS], F32, tag="bank")
             for s in range(MATS):
                 multiply(acc[:, s, :], s, h * HALF_TILES + i, c_codes[q], c_scales[q])
-            empty_bank(i)(
+            empty_bank(turn)(
                 out=out_sb[h][
                     :, q * CHUNK_B : (q + 1) * CHUNK_B, i * MATS : (i + 1) * MATS, D_IN:D_CAND
                 ].rearrange("p b s c -> p s b c"),
@@ -220,7 +220,7 @@ def tile_agcrnlayer_pb_kernel(tc, adj, cheb2, x, state, r_logit, out):
                         gate_product(gate[0], gate[1])
                     elif i == 3:
                         gate_quantise(gate[0], gate[1])
-                chunk_bank(q, h, i)
+                chunk_bank(q, h, i, i if gate is None or i == 1 else 0)
             if with_x:
                 x_banks(h)
             store(q, h)
@@ -247,7 +247,7 @@ def tile_agcrnlayer_pb_kernel(tc, adj, cheb2, x, state, r_logit, out):
             gate_sigmoid(1, g)
             gate_product(1, g)
         for i in range(HALF_TILES):
-            chunk_bank(0, 0, i)
+            chunk_bank(0, 0, i, i)
         for g in range(PASSES):
             gate_quantise(1, g)
         for g in range(PASSES):

@@ -51,7 +51,8 @@ def tile_agcrnlayer_pb_kernel(tc, adj, cheb2, x, state, r_logit, out):
         a_codes = keep.tile([P, MATS, ROW_TILES, PASSES, P], U32, align_bytes=64)
         a_scales = keep.tile([P, MATS, ROW_TILES, PASSES, P], U8, align_bytes=64)
 
-        x_raw = keep.tile([P, PASSES, BATCH, PACK * D_IN], BF16)
+        x_rows = keep.tile([P, BATCH, PASSES * PACK * D_IN], BF16)
+        spread = keep.tile([P, PASSES, PASSES, P], BF16)
         x_grouped = keep.tile([P, PASSES, BATCH, D_IN, PACK], BF16, align_bytes=64)
         x_codes = keep.tile([P, PASSES, X_COLS], U32, align_bytes=64)
         x_scales = keep.tile([P, PASSES, X_COLS], U8, align_bytes=64)
@@ -226,12 +227,20 @@ def tile_agcrnlayer_pb_kernel(tc, adj, cheb2, x, state, r_logit, out):
             store(q, h)
 
         make_identity(nc, ident[:])
+        nc.gpsimd.memset(spread[:], 0.0)
+        for g in range(PASSES):
+            for e in range(PASSES):
+                nc.gpsimd.tensor_copy(
+                    out=spread[:, g, e, e:P:PASSES],
+                    in_=ident[:, g * (P // PASSES) : (g + 1) * (P // PASSES)],
+                )
 
         load_chunk(0)
         load_matrices(0)
         load_chunk(1)
-        for g in range(PASSES):
-            load_pass(x_raw[:, g], x, g)
+        nc.sync.dma_start(
+            out=x_rows[:], in_=x.rearrange("b (q r) c -> q b (r c)", r=PASSES * PACK)
+        )
         load_matrices(1)
         load_chunk(2)
         load_chunk(3)
@@ -251,7 +260,16 @@ def tile_agcrnlayer_pb_kernel(tc, adj, cheb2, x, state, r_logit, out):
         for g in range(PASSES):
             gate_quantise(1, g)
         for g in range(PASSES):
-            nc.vector.tensor_copy(out=x_grouped[:, g], in_=words_side_by_side(x_raw[:, g]))
+            moved = psum.tile([P, BATCH, PACK * D_IN], F32, tag="bank")
+            for e in range(PASSES):
+                nc.tensor.matmul(
+                    moved[:],
+                    lhsT=spread[:, g, e, :],
+                    rhs=x_rows[:, :, e * PACK * D_IN : (e + 1) * PACK * D_IN],
+                    start=(e == 0),
+                    stop=(e == PASSES - 1),
+                )
+            nc.scalar.copy(out=x_grouped[:, g], in_=words_side_by_side(moved[:]))
         nc.vector.quantize_mx(
             out=x_codes[:].rearrange("p g w -> p (g w)").bitcast(FP8X4),
             scales=x_scales[:].rearrange("p g w -> p (g w)"),

@@ -29,8 +29,12 @@ X_COLS = BATCH * D_IN
 CHUNK_B = 4
 CHUNKS = BATCH // CHUNK_B
 CHUNK_COLS = CHUNK_B * D_STATE
+PAIR_B = 2
+PAIR_COLS = PAIR_B * D_STATE
 BANK_F32 = 512
 X_GROUPS = BANK_F32 // X_COLS
+PAIR_ROWS = BANK_F32 // PAIR_COLS
+PAIR_BANKS = ROW_TILES * MATS // PAIR_ROWS
 PSUM_BANKS = 8
 
 FLOPS = 2 * MATS * NODES * NODES * BATCH * D_CAND
@@ -68,10 +72,7 @@ def tile_agcrnlayer_pb_kernel(tc, adj, cheb2, x, state, r_logit, out):
             keep.tile([P, PASSES, CHUNK_COLS], U8, name="c_scales%d" % q, align_bytes=64)
             for q in range(CHUNKS)
         ]
-        out_sb = [
-            keep.tile([P, BATCH, HALF_ROWS, D_CAND], F32, name="out_sb%d" % h)
-            for h in range(HALVES)
-        ]
+        out_sb = keep.tile([P, BATCH, ROW_TILES * MATS, D_CAND], F32)
         gates = {}
         cands = {}
         waiting = []
@@ -182,34 +183,59 @@ def tile_agcrnlayer_pb_kernel(tc, adj, cheb2, x, state, r_logit, out):
             for s in range(MATS):
                 multiply(acc[:, s, :], s, h * HALF_TILES + i, c_codes[q], c_scales[q])
             empty_bank(turn)(
-                out=out_sb[h][
-                    :, q * CHUNK_B : (q + 1) * CHUNK_B, i * MATS : (i + 1) * MATS, D_IN:D_CAND
+                out=out_sb[
+                    :,
+                    q * CHUNK_B : (q + 1) * CHUNK_B,
+                    h * HALF_ROWS + i * MATS : h * HALF_ROWS + (i + 1) * MATS,
+                    D_IN:D_CAND,
                 ].rearrange("p b s c -> p s b c"),
                 in_=acc[:].rearrange("p s (b c) -> p s b c", c=D_STATE),
             )
 
         def x_banks(h):
-            for first_row in range(0, HALF_ROWS, X_GROUPS):
+            for first_row in range(h * HALF_ROWS, (h + 1) * HALF_ROWS, X_GROUPS):
                 acc = psum.tile([P, X_GROUPS, X_COLS], F32, tag="bank")
                 for i in range(X_GROUPS):
                     row = first_row + i
-                    multiply(
-                        acc[:, i, :], row % MATS, h * HALF_TILES + row // MATS, x_codes, x_scales
-                    )
+                    multiply(acc[:, i, :], row % MATS, row // MATS, x_codes, x_scales)
                 empty_bank(first_row // X_GROUPS)(
-                    out=out_sb[h][:, :, first_row : first_row + X_GROUPS, 0:D_IN].rearrange(
+                    out=out_sb[:, :, first_row : first_row + X_GROUPS, 0:D_IN].rearrange(
                         "p b r c -> p r b c"
                     ),
                     in_=acc[:].rearrange("p r (b c) -> p r b c", c=D_IN),
                 )
 
-        def store(q, h):
-            batches = slice(q * CHUNK_B, (q + 1) * CHUNK_B)
+        def pair_bank(q, a, k, turn):
+            first_b = q * CHUNK_B + a * PAIR_B
+            cols = slice(a * PAIR_COLS, (a + 1) * PAIR_COLS)
+            rows = slice(k * PAIR_ROWS, (k + 1) * PAIR_ROWS)
+            acc = psum.tile([P, PAIR_ROWS, PAIR_COLS], F32, tag="bank")
+            for i in range(PAIR_ROWS):
+                row = k * PAIR_ROWS + i
+                multiply(
+                    acc[:, i, :],
+                    row % MATS,
+                    row // MATS,
+                    c_codes[q][:, :, cols],
+                    c_scales[q][:, :, cols],
+                )
+            empty_bank(turn)(
+                out=out_sb[:, first_b : first_b + PAIR_B, rows, D_IN:D_CAND].rearrange(
+                    "p b r c -> p r b c"
+                ),
+                in_=acc[:].rearrange("p r (b c) -> p r b c", c=D_STATE),
+            )
+
+        def store(first_b, count, h=None):
+            batches = slice(first_b, first_b + count)
+            rows = slice(0, ROW_TILES) if h is None else slice(h * HALF_TILES, (h + 1) * HALF_TILES)
             nc.sync.dma_start(
                 out=out[batches].rearrange("b (p j) s c -> p b j (s c)", j=ROW_TILES)[
-                    :, :, h * HALF_TILES : (h + 1) * HALF_TILES, :
+                    :, :, rows, :
                 ],
-                in_=out_sb[h][:, batches].rearrange("p b (i s) c -> p b i (s c)", s=MATS),
+                in_=out_sb[:, batches].rearrange("p b (j s) c -> p b j (s c)", s=MATS)[
+                    :, :, rows, :
+                ],
             )
 
         def chunk_half(q, h, gate=None, with_x=False):
@@ -224,7 +250,19 @@ def tile_agcrnlayer_pb_kernel(tc, adj, cheb2, x, state, r_logit, out):
                 chunk_bank(q, h, i, i if gate is None or i == 1 else 0)
             if with_x:
                 x_banks(h)
-            store(q, h)
+            store(q * CHUNK_B, CHUNK_B, h)
+
+        def chunk_pair(q, a, gate=None):
+            for k in range(PAIR_BANKS):
+                if gate is not None:
+                    if k == 0:
+                        gate_sigmoid(gate[0], gate[1])
+                    elif k == 1:
+                        gate_product(gate[0], gate[1])
+                    elif k == 3:
+                        gate_quantise(gate[0], gate[1])
+                pair_bank(q, a, k, k if gate is None or k == 1 else 0)
+            store(q * CHUNK_B + a * PAIR_B, PAIR_B)
 
         make_identity(nc, ident[:])
         nc.gpsimd.memset(spread[:], 0.0)
@@ -278,11 +316,11 @@ def tile_agcrnlayer_pb_kernel(tc, adj, cheb2, x, state, r_logit, out):
 
         transpose_half(1)
         x_banks(0)
-        store(0, 0)
+        store(0, CHUNK_B, 0)
         chunk_half(1, 0, gate=(2, 0))
         chunk_half(0, 1, gate=(2, 1), with_x=True)
         chunk_half(1, 1, gate=(3, 0))
-        chunk_half(2, 0, gate=(3, 1))
-        chunk_half(2, 1)
-        chunk_half(3, 0)
-        chunk_half(3, 1)
+        chunk_pair(2, 0, gate=(3, 1))
+        chunk_pair(2, 1)
+        chunk_pair(3, 0)
+        chunk_pair(3, 1)

@@ -126,16 +126,18 @@ def tile_agcrnlayer_pb_kernel(tc, adj, cheb2, x, state, r_logit, out):
                 in_=cands[q][:, g].rearrange("p b c t -> p (b c t)"),
             )
 
+        def copier(engine):
+            return nc.vector.tensor_copy if engine == "V" else nc.scalar.copy
+
         def quantise_waiting():
-            s, j, grouped = waiting[0]
-            waiting.clear()
+            s, j, grouped = waiting.pop()
             nc.vector.quantize_mx(
                 out=a_codes[:, s, j].rearrange("p g m -> p (g m)").bitcast(FP8X4),
                 scales=a_scales[:, s, j].rearrange("p g m -> p (g m)"),
                 in_=grouped[:].rearrange("p g m t -> p (g m t)"),
             )
 
-        def transpose_tile(s, j, turn):
+        def transpose_tile(s, j, engine):
             words = mat_sb[s][:].bitcast(F32)
             flipped = psum.tile([P, PASSES, PAIRS, P], F32, tag="bank")
             for g in range(PASSES):
@@ -147,21 +149,12 @@ def tile_agcrnlayer_pb_kernel(tc, adj, cheb2, x, state, r_logit, out):
                         ident[:],
                     )
             grouped = flip.tile([P, PASSES, P, PACK], BF16, align_bytes=64)
-            (nc.vector.tensor_copy if turn % 4 == 3 else nc.scalar.copy)(
+            copier(engine)(
                 out=grouped[:].bitcast(F32), in_=flipped[:].rearrange("p g u m -> p g m u")
             )
             if waiting:
                 quantise_waiting()
             waiting.append((s, j, grouped))
-
-        def transpose_half(h):
-            turn = 0
-            for j in range(h * HALF_TILES, (h + 1) * HALF_TILES, LOAD_TILES):
-                for s in range(MATS):
-                    for k in range(LOAD_TILES):
-                        transpose_tile(s, j + k, turn)
-                        turn += 1
-            quantise_waiting()
 
         def multiply(acc, s, j, codes, scales):
             for g in range(PASSES):
@@ -175,37 +168,18 @@ def tile_agcrnlayer_pb_kernel(tc, adj, cheb2, x, state, r_logit, out):
                     stop=(g == PASSES - 1),
                 )
 
-        def empty_bank(turn):
-            return nc.scalar.copy if turn % 2 == 0 else nc.vector.tensor_copy
-
-        def chunk_bank(q, h, i, turn):
+        def chunk_bank(q, j, engine):
             acc = psum.tile([P, MATS, CHUNK_COLS], F32, tag="bank")
             for s in range(MATS):
-                multiply(acc[:, s, :], s, h * HALF_TILES + i, c_codes[q], c_scales[q])
-            empty_bank(turn)(
+                multiply(acc[:, s, :], s, j, c_codes[q], c_scales[q])
+            copier(engine)(
                 out=out_sb[
-                    :,
-                    q * CHUNK_B : (q + 1) * CHUNK_B,
-                    h * HALF_ROWS + i * MATS : h * HALF_ROWS + (i + 1) * MATS,
-                    D_IN:D_CAND,
+                    :, q * CHUNK_B : (q + 1) * CHUNK_B, j * MATS : (j + 1) * MATS, D_IN:D_CAND
                 ].rearrange("p b s c -> p s b c"),
                 in_=acc[:].rearrange("p s (b c) -> p s b c", c=D_STATE),
             )
 
-        def x_banks(h):
-            for first_row in range(h * HALF_ROWS, (h + 1) * HALF_ROWS, X_GROUPS):
-                acc = psum.tile([P, X_GROUPS, X_COLS], F32, tag="bank")
-                for i in range(X_GROUPS):
-                    row = first_row + i
-                    multiply(acc[:, i, :], row % MATS, row // MATS, x_codes, x_scales)
-                empty_bank(first_row // X_GROUPS)(
-                    out=out_sb[:, :, first_row : first_row + X_GROUPS, 0:D_IN].rearrange(
-                        "p b r c -> p r b c"
-                    ),
-                    in_=acc[:].rearrange("p r (b c) -> p r b c", c=D_IN),
-                )
-
-        def pair_bank(q, a, k, turn):
+        def pair_bank(q, a, k, engine):
             first_b = q * CHUNK_B + a * PAIR_B
             cols = slice(a * PAIR_COLS, (a + 1) * PAIR_COLS)
             rows = slice(k * PAIR_ROWS, (k + 1) * PAIR_ROWS)
@@ -219,11 +193,43 @@ def tile_agcrnlayer_pb_kernel(tc, adj, cheb2, x, state, r_logit, out):
                     c_codes[q][:, :, cols],
                     c_scales[q][:, :, cols],
                 )
-            empty_bank(turn)(
+            copier(engine)(
                 out=out_sb[:, first_b : first_b + PAIR_B, rows, D_IN:D_CAND].rearrange(
                     "p b r c -> p r b c"
                 ),
                 in_=acc[:].rearrange("p r (b c) -> p r b c", c=D_STATE),
+            )
+
+        def x_words(g, engine):
+            moved = psum.tile([P, BATCH, PACK * D_IN], F32, tag="bank")
+            for e in range(PASSES):
+                nc.tensor.matmul(
+                    moved[:],
+                    lhsT=spread[:, g, e, :],
+                    rhs=x_rows[:, :, e * PACK * D_IN : (e + 1) * PACK * D_IN],
+                    start=(e == 0),
+                    stop=(e == PASSES - 1),
+                )
+            copier(engine)(out=x_grouped[:, g], in_=words_side_by_side(moved[:]))
+
+        def x_quantise():
+            nc.vector.quantize_mx(
+                out=x_codes[:].rearrange("p g w -> p (g w)").bitcast(FP8X4),
+                scales=x_scales[:].rearrange("p g w -> p (g w)"),
+                in_=x_grouped[:].rearrange("p g b c t -> p (g b c t)"),
+            )
+
+        def x_bank(k, engine):
+            first_row = k * X_GROUPS
+            acc = psum.tile([P, X_GROUPS, X_COLS], F32, tag="bank")
+            for i in range(X_GROUPS):
+                row = first_row + i
+                multiply(acc[:, i, :], row % MATS, row // MATS, x_codes, x_scales)
+            copier(engine)(
+                out=out_sb[:, :, first_row : first_row + X_GROUPS, 0:D_IN].rearrange(
+                    "p b r c -> p r b c"
+                ),
+                in_=acc[:].rearrange("p r (b c) -> p r b c", c=D_IN),
             )
 
         def store(first_b, count, h=None):
@@ -237,32 +243,6 @@ def tile_agcrnlayer_pb_kernel(tc, adj, cheb2, x, state, r_logit, out):
                     :, :, rows, :
                 ],
             )
-
-        def chunk_half(q, h, gate=None, with_x=False):
-            for i in range(HALF_TILES):
-                if gate is not None:
-                    if i == 0:
-                        gate_sigmoid(gate[0], gate[1])
-                    elif i == 1:
-                        gate_product(gate[0], gate[1])
-                    elif i == 3:
-                        gate_quantise(gate[0], gate[1])
-                chunk_bank(q, h, i, i if gate is None or i == 1 else 0)
-            if with_x:
-                x_banks(h)
-            store(q * CHUNK_B, CHUNK_B, h)
-
-        def chunk_pair(q, a, gate=None):
-            for k in range(PAIR_BANKS):
-                if gate is not None:
-                    if k == 0:
-                        gate_sigmoid(gate[0], gate[1])
-                    elif k == 1:
-                        gate_product(gate[0], gate[1])
-                    elif k == 3:
-                        gate_quantise(gate[0], gate[1])
-                pair_bank(q, a, k, k if gate is None or k == 1 else 0)
-            store(q * CHUNK_B + a * PAIR_B, PAIR_B)
 
         make_identity(nc, ident[:])
         nc.gpsimd.memset(spread[:], 0.0)
@@ -289,38 +269,83 @@ def tile_agcrnlayer_pb_kernel(tc, adj, cheb2, x, state, r_logit, out):
         for g in range(PASSES):
             gate_quantise(0, g)
 
-        transpose_half(0)
-        for g in range(PASSES):
-            gate_sigmoid(1, g)
-            gate_product(1, g)
-        for i in range(HALF_TILES):
-            chunk_bank(0, 0, i, i)
-        for g in range(PASSES):
-            gate_quantise(1, g)
-        for g in range(PASSES):
-            moved = psum.tile([P, BATCH, PACK * D_IN], F32, tag="bank")
-            for e in range(PASSES):
-                nc.tensor.matmul(
-                    moved[:],
-                    lhsT=spread[:, g, e, :],
-                    rhs=x_rows[:, :, e * PACK * D_IN : (e + 1) * PACK * D_IN],
-                    start=(e == 0),
-                    stop=(e == PASSES - 1),
-                )
-            nc.scalar.copy(out=x_grouped[:, g], in_=words_side_by_side(moved[:]))
-        nc.vector.quantize_mx(
-            out=x_codes[:].rearrange("p g w -> p (g w)").bitcast(FP8X4),
-            scales=x_scales[:].rearrange("p g w -> p (g w)"),
-            in_=x_grouped[:].rearrange("p g b c t -> p (g b c t)"),
-        )
+        def transpose_tiles(j, engines):
+            for k in range(LOAD_TILES * MATS):
+                transpose_tile(k // LOAD_TILES, j + k % LOAD_TILES, engines[k])
 
-        transpose_half(1)
-        x_banks(0)
+        transpose_tiles(0, "SSSV")
+        quantise_waiting()
+        transpose_tiles(2, "SSSV")
+        quantise_waiting()
+
+        chunk_bank(0, 0, "V")
+        gate_sigmoid(1, 0)
+        chunk_bank(0, 1, "V")
+        gate_sigmoid(1, 1)
+        chunk_bank(0, 2, "S")
+        chunk_bank(0, 3, "S")
+        gate_product(1, 0)
+        x_words(0, "V")
+        gate_product(1, 1)
+        x_words(1, "S")
+        x_quantise()
+
+        transpose_tile(0, 4, "S")
+        gate_quantise(1, 0)
+        gate_quantise(1, 1)
+        transpose_tile(0, 5, "S")
+        transpose_tile(1, 4, "S")
+        transpose_tile(1, 5, "S")
+        quantise_waiting()
+        transpose_tiles(6, "SSSV")
+        quantise_waiting()
+        x_bank(0, "S")
+        x_bank(1, "S")
         store(0, CHUNK_B, 0)
-        chunk_half(1, 0, gate=(2, 0))
-        chunk_half(0, 1, gate=(2, 1), with_x=True)
-        chunk_half(1, 1, gate=(3, 0))
-        chunk_pair(2, 0, gate=(3, 1))
-        chunk_pair(2, 1)
-        chunk_pair(3, 0)
-        chunk_pair(3, 1)
+
+        gate_sigmoid(2, 0)
+        chunk_bank(1, 0, "V")
+        gate_sigmoid(2, 1)
+        chunk_bank(1, 1, "V")
+        chunk_bank(1, 2, "V")
+        chunk_bank(1, 3, "S")
+        store(CHUNK_B, CHUNK_B, 0)
+
+        chunk_bank(0, 4, "V")
+        chunk_bank(0, 5, "S")
+        chunk_bank(0, 6, "S")
+        gate_product(2, 0)
+        chunk_bank(0, 7, "S")
+        x_bank(2, "V")
+        gate_product(2, 1)
+        x_bank(3, "S")
+        store(0, CHUNK_B, 1)
+
+        gate_quantise(2, 0)
+        gate_quantise(2, 1)
+        chunk_bank(1, 4, "S")
+        gate_sigmoid(3, 0)
+        chunk_bank(1, 5, "S")
+        chunk_bank(1, 6, "S")
+        chunk_bank(1, 7, "V")
+        store(CHUNK_B, CHUNK_B, 1)
+
+        gate_sigmoid(3, 1)
+        pair_bank(2, 0, 0, "S")
+        gate_product(3, 0)
+        pair_bank(2, 0, 1, "V")
+        pair_bank(2, 0, 2, "S")
+        gate_product(3, 1)
+        pair_bank(2, 0, 3, "S")
+        store(2 * CHUNK_B, PAIR_B)
+        pair_bank(2, 1, 0, "S")
+        gate_quantise(3, 0)
+        pair_bank(2, 1, 1, "S")
+        gate_quantise(3, 1)
+        pair_bank(2, 1, 2, "S")
+        pair_bank(2, 1, 3, "V")
+        store(2 * CHUNK_B + PAIR_B, PAIR_B)
+        for a in range(PASSES):
+            for k in range(PAIR_BANKS):
+                pair_bank(3, a, k, "VS"[k % 2])
+            store(3 * CHUNK_B + a * PAIR_B, PAIR_B)

@@ -232,10 +232,10 @@ def tile_agcrnlayer_pb_kernel(tc, adj, cheb2, x, state, r_logit, out):
                 in_=acc[:].rearrange("p r (b c) -> p r b c", c=D_IN),
             )
 
-        def store(first_b, count, h=None):
+        def store(queue, first_b, count, h=None):
             batches = slice(first_b, first_b + count)
             rows = slice(0, ROW_TILES) if h is None else slice(h * HALF_TILES, (h + 1) * HALF_TILES)
-            nc.sync.dma_start(
+            queue.dma_start(
                 out=out[batches].rearrange("b (p j) s c -> p b j (s c)", j=ROW_TILES)[
                     :, :, rows, :
                 ],
@@ -301,7 +301,7 @@ def tile_agcrnlayer_pb_kernel(tc, adj, cheb2, x, state, r_logit, out):
         quantise_waiting()
         x_bank(0, "S")
         x_bank(1, "S")
-        store(0, CHUNK_B, 0)
+        store(nc.sync, 0, CHUNK_B, 0)
 
         gate_sigmoid(2, 0)
         chunk_bank(1, 0, "V")
@@ -309,17 +309,17 @@ def tile_agcrnlayer_pb_kernel(tc, adj, cheb2, x, state, r_logit, out):
         chunk_bank(1, 1, "V")
         chunk_bank(1, 2, "V")
         chunk_bank(1, 3, "S")
-        store(CHUNK_B, CHUNK_B, 0)
 
         chunk_bank(0, 4, "V")
         chunk_bank(0, 5, "S")
+        store(nc.scalar, CHUNK_B, CHUNK_B, 0)
         chunk_bank(0, 6, "S")
         gate_product(2, 0)
         chunk_bank(0, 7, "S")
         x_bank(2, "V")
         gate_product(2, 1)
         x_bank(3, "S")
-        store(0, CHUNK_B, 1)
+        store(nc.sync, 0, CHUNK_B, 1)
 
         gate_quantise(2, 0)
         gate_quantise(2, 1)
@@ -328,24 +328,28 @@ def tile_agcrnlayer_pb_kernel(tc, adj, cheb2, x, state, r_logit, out):
         chunk_bank(1, 5, "S")
         chunk_bank(1, 6, "S")
         chunk_bank(1, 7, "V")
-        store(CHUNK_B, CHUNK_B, 1)
 
         gate_sigmoid(3, 1)
         pair_bank(2, 0, 0, "S")
+        store(nc.scalar, CHUNK_B, CHUNK_B, 1)
         gate_product(3, 0)
         pair_bank(2, 0, 1, "V")
         pair_bank(2, 0, 2, "S")
         gate_product(3, 1)
         pair_bank(2, 0, 3, "S")
-        store(2 * CHUNK_B, PAIR_B)
+        store(nc.sync, 2 * CHUNK_B, PAIR_B)
         pair_bank(2, 1, 0, "S")
         gate_quantise(3, 0)
         pair_bank(2, 1, 1, "S")
         gate_quantise(3, 1)
         pair_bank(2, 1, 2, "S")
         pair_bank(2, 1, 3, "V")
-        store(2 * CHUNK_B + PAIR_B, PAIR_B)
-        for a in range(PASSES):
-            for k in range(PAIR_BANKS):
-                pair_bank(3, a, k, "VS"[k % 2])
-            store(3 * CHUNK_B + a * PAIR_B, PAIR_B)
+        pair_bank(3, 0, 0, "V")
+        pair_bank(3, 0, 1, "S")
+        store(nc.scalar, 2 * CHUNK_B + PAIR_B, PAIR_B)
+        pair_bank(3, 0, 2, "V")
+        pair_bank(3, 0, 3, "S")
+        store(nc.sync, 3 * CHUNK_B, PAIR_B)
+        for k in range(PAIR_BANKS):
+            pair_bank(3, 1, k, "VS"[k % 2])
+        store(nc.scalar, 3 * CHUNK_B + PAIR_B, PAIR_B)

@@ -233,6 +233,9 @@ def tile_agcrnlayer_pb_kernel(tc, adj, cheb2, x, state, r_logit, out):
             )
 
         def store(queue, first_b, count, h=None):
+            if queue is nc.scalar:
+                first_b += count // 2
+            count //= 2
             batches = slice(first_b, first_b + count)
             rows = slice(0, ROW_TILES) if h is None else slice(h * HALF_TILES, (h + 1) * HALF_TILES)
             queue.dma_start(
@@ -302,6 +305,7 @@ def tile_agcrnlayer_pb_kernel(tc, adj, cheb2, x, state, r_logit, out):
         x_bank(0, "S")
         x_bank(1, "S")
         store(nc.sync, 0, CHUNK_B, 0)
+        store(nc.scalar, 0, CHUNK_B, 0)
 
         gate_sigmoid(2, 0)
         chunk_bank(1, 0, "V")
@@ -309,6 +313,7 @@ def tile_agcrnlayer_pb_kernel(tc, adj, cheb2, x, state, r_logit, out):
         chunk_bank(1, 1, "V")
         chunk_bank(1, 2, "V")
         chunk_bank(1, 3, "S")
+        store(nc.sync, CHUNK_B, CHUNK_B, 0)
 
         chunk_bank(0, 4, "V")
         chunk_bank(0, 5, "S")
@@ -320,6 +325,7 @@ def tile_agcrnlayer_pb_kernel(tc, adj, cheb2, x, state, r_logit, out):
         gate_product(2, 1)
         x_bank(3, "S")
         store(nc.sync, 0, CHUNK_B, 1)
+        store(nc.scalar, 0, CHUNK_B, 1)
 
         gate_quantise(2, 0)
         gate_quantise(2, 1)
@@ -328,6 +334,7 @@ def tile_agcrnlayer_pb_kernel(tc, adj, cheb2, x, state, r_logit, out):
         chunk_bank(1, 5, "S")
         chunk_bank(1, 6, "S")
         chunk_bank(1, 7, "V")
+        store(nc.sync, CHUNK_B, CHUNK_B, 1)
 
         gate_sigmoid(3, 1)
         pair_bank(2, 0, 0, "S")
@@ -338,18 +345,22 @@ def tile_agcrnlayer_pb_kernel(tc, adj, cheb2, x, state, r_logit, out):
         gate_product(3, 1)
         pair_bank(2, 0, 3, "S")
         store(nc.sync, 2 * CHUNK_B, PAIR_B)
+        store(nc.scalar, 2 * CHUNK_B, PAIR_B)
         pair_bank(2, 1, 0, "S")
         gate_quantise(3, 0)
         pair_bank(2, 1, 1, "S")
         gate_quantise(3, 1)
         pair_bank(2, 1, 2, "S")
         pair_bank(2, 1, 3, "V")
+        store(nc.sync, 2 * CHUNK_B + PAIR_B, PAIR_B)
         pair_bank(3, 0, 0, "V")
         pair_bank(3, 0, 1, "S")
         store(nc.scalar, 2 * CHUNK_B + PAIR_B, PAIR_B)
         pair_bank(3, 0, 2, "V")
         pair_bank(3, 0, 3, "S")
         store(nc.sync, 3 * CHUNK_B, PAIR_B)
+        store(nc.scalar, 3 * CHUNK_B, PAIR_B)
         for k in range(PAIR_BANKS):
             pair_bank(3, 1, k, "VS"[k % 2])
+        store(nc.sync, 3 * CHUNK_B + PAIR_B, PAIR_B)
         store(nc.scalar, 3 * CHUNK_B + PAIR_B, PAIR_B)

@@ -168,17 +168,6 @@ def tile_agcrnlayer_pb_kernel(tc, adj, cheb2, x, state, r_logit, out):
                     stop=(g == PASSES - 1),
                 )
 
-        def chunk_bank(q, j, engine):
-            acc = psum.tile([P, MATS, CHUNK_COLS], F32, tag="bank")
-            for s in range(MATS):
-                multiply(acc[:, s, :], s, j, c_codes[q], c_scales[q])
-            copier(engine)(
-                out=out_sb[
-                    :, q * CHUNK_B : (q + 1) * CHUNK_B, j * MATS : (j + 1) * MATS, D_IN:D_CAND
-                ].rearrange("p b s c -> p s b c"),
-                in_=acc[:].rearrange("p s (b c) -> p s b c", c=D_STATE),
-            )
-
         def pair_bank(q, a, k, engine):
             first_b = q * CHUNK_B + a * PAIR_B
             cols = slice(a * PAIR_COLS, (a + 1) * PAIR_COLS)
@@ -232,19 +221,10 @@ def tile_agcrnlayer_pb_kernel(tc, adj, cheb2, x, state, r_logit, out):
                 in_=acc[:].rearrange("p r (b c) -> p r b c", c=D_IN),
             )
 
-        def store(queue, first_b, count, h=None):
-            if queue is nc.scalar:
-                first_b += count // 2
-            count //= 2
-            batches = slice(first_b, first_b + count)
-            rows = slice(0, ROW_TILES) if h is None else slice(h * HALF_TILES, (h + 1) * HALF_TILES)
+        def store(queue, b):
             queue.dma_start(
-                out=out[batches].rearrange("b (p j) s c -> p b j (s c)", j=ROW_TILES)[
-                    :, :, rows, :
-                ],
-                in_=out_sb[:, batches].rearrange("p b (j s) c -> p b j (s c)", s=MATS)[
-                    :, :, rows, :
-                ],
+                out=out[b].rearrange("(p j) s c -> p (j s c)", j=ROW_TILES),
+                in_=out_sb[:, b].rearrange("p r c -> p (r c)"),
             )
 
         make_identity(nc, ident[:])
@@ -258,11 +238,11 @@ def tile_agcrnlayer_pb_kernel(tc, adj, cheb2, x, state, r_logit, out):
 
         load_chunk(0)
         load_matrices(0)
-        load_chunk(1)
+        load_matrices(1)
         nc.sync.dma_start(
             out=x_rows[:], in_=x.rearrange("b (q r) c -> q b (r c)", r=PASSES * PACK)
         )
-        load_matrices(1)
+        load_chunk(1)
         load_chunk(2)
         load_chunk(3)
 
@@ -272,95 +252,64 @@ def tile_agcrnlayer_pb_kernel(tc, adj, cheb2, x, state, r_logit, out):
         for g in range(PASSES):
             gate_quantise(0, g)
 
-        def transpose_tiles(j, engines):
-            for k in range(LOAD_TILES * MATS):
-                transpose_tile(k // LOAD_TILES, j + k % LOAD_TILES, engines[k])
+        for j in range(0, ROW_TILES, LOAD_TILES):
+            for s in range(MATS):
+                for k in range(LOAD_TILES):
+                    last_of_load = (s, k) == (MATS - 1, LOAD_TILES - 1)
+                    if last_of_load and j == ROW_TILES - LOAD_TILES:
+                        gate_sigmoid(1, 0)
+                    transpose_tile(s, j + k, "V" if last_of_load and j > 0 else "S")
+            quantise_waiting()
 
-        transpose_tiles(0, "SSSV")
-        quantise_waiting()
-        transpose_tiles(2, "SSSV")
-        quantise_waiting()
-
-        chunk_bank(0, 0, "V")
-        gate_sigmoid(1, 0)
-        chunk_bank(0, 1, "V")
+        x_words(0, "S")
         gate_sigmoid(1, 1)
-        chunk_bank(0, 2, "S")
-        chunk_bank(0, 3, "S")
-        gate_product(1, 0)
-        x_words(0, "V")
-        gate_product(1, 1)
-        x_words(1, "S")
+        x_words(1, "V")
         x_quantise()
 
-        transpose_tile(0, 4, "S")
-        gate_quantise(1, 0)
-        gate_quantise(1, 1)
-        transpose_tile(0, 5, "S")
-        transpose_tile(1, 4, "S")
-        transpose_tile(1, 5, "S")
-        quantise_waiting()
-        transpose_tiles(6, "SSSV")
-        quantise_waiting()
-        x_bank(0, "S")
-        x_bank(1, "S")
-        store(nc.sync, 0, CHUNK_B, 0)
-        store(nc.scalar, 0, CHUNK_B, 0)
-
-        gate_sigmoid(2, 0)
-        chunk_bank(1, 0, "V")
-        gate_sigmoid(2, 1)
-        chunk_bank(1, 1, "V")
-        chunk_bank(1, 2, "V")
-        chunk_bank(1, 3, "S")
-        store(nc.sync, CHUNK_B, CHUNK_B, 0)
-
-        chunk_bank(0, 4, "V")
-        chunk_bank(0, 5, "S")
-        store(nc.scalar, CHUNK_B, CHUNK_B, 0)
-        chunk_bank(0, 6, "S")
-        gate_product(2, 0)
-        chunk_bank(0, 7, "S")
-        x_bank(2, "V")
-        gate_product(2, 1)
-        x_bank(3, "S")
-        store(nc.sync, 0, CHUNK_B, 1)
-        store(nc.scalar, 0, CHUNK_B, 1)
-
-        gate_quantise(2, 0)
-        gate_quantise(2, 1)
-        chunk_bank(1, 4, "S")
-        gate_sigmoid(3, 0)
-        chunk_bank(1, 5, "S")
-        chunk_bank(1, 6, "S")
-        chunk_bank(1, 7, "V")
-        store(nc.sync, CHUNK_B, CHUNK_B, 1)
-
-        gate_sigmoid(3, 1)
-        pair_bank(2, 0, 0, "S")
-        store(nc.scalar, CHUNK_B, CHUNK_B, 1)
-        gate_product(3, 0)
-        pair_bank(2, 0, 1, "V")
-        pair_bank(2, 0, 2, "S")
-        gate_product(3, 1)
-        pair_bank(2, 0, 3, "S")
-        store(nc.sync, 2 * CHUNK_B, PAIR_B)
-        store(nc.scalar, 2 * CHUNK_B, PAIR_B)
-        pair_bank(2, 1, 0, "S")
-        gate_quantise(3, 0)
-        pair_bank(2, 1, 1, "S")
-        gate_quantise(3, 1)
-        pair_bank(2, 1, 2, "S")
-        pair_bank(2, 1, 3, "V")
-        store(nc.sync, 2 * CHUNK_B + PAIR_B, PAIR_B)
-        pair_bank(3, 0, 0, "V")
-        pair_bank(3, 0, 1, "S")
-        store(nc.scalar, 2 * CHUNK_B + PAIR_B, PAIR_B)
-        pair_bank(3, 0, 2, "V")
-        pair_bank(3, 0, 3, "S")
-        store(nc.sync, 3 * CHUNK_B, PAIR_B)
-        store(nc.scalar, 3 * CHUNK_B, PAIR_B)
         for k in range(PAIR_BANKS):
-            pair_bank(3, 1, k, "VS"[k % 2])
-        store(nc.sync, 3 * CHUNK_B + PAIR_B, PAIR_B)
-        store(nc.scalar, 3 * CHUNK_B + PAIR_B, PAIR_B)
+            if k == PAIR_BANKS - 1:
+                gate_product(1, 0)
+            pair_bank(0, 0, k, "S")
+        gate_product(1, 1)
+        x_bank(0, "V")
+        x_bank(1, "S")
+        x_bank(2, "S")
+        gate_quantise(1, 0)
+        x_bank(3, "V")
+        store(nc.sync, 0)
+        gate_sigmoid(2, 0)
+        gate_quantise(1, 1)
+        pair_bank(0, 1, 0, "S")
+        store(nc.scalar, 1)
+        for k in range(1, PAIR_BANKS):
+            pair_bank(0, 1, k, "V")
+        store(nc.sync, 2)
+
+        for q in range(1, CHUNKS - 1):
+            gate_sigmoid(q + 1, 1)
+            pair_bank(q, 0, 0, "S")
+            store(nc.scalar, q * CHUNK_B - 1)
+            gate_product(q + 1, 0)
+            pair_bank(q, 0, 1, "S")
+            gate_product(q + 1, 1)
+            pair_bank(q, 0, 2, "S")
+            gate_quantise(q + 1, 0)
+            pair_bank(q, 0, 3, "S")
+            store(nc.sync, q * CHUNK_B)
+            store(nc.scalar, q * CHUNK_B + 1)
+            if q + 2 < CHUNKS:
+                gate_sigmoid(q + 2, 0)
+            gate_quantise(q + 1, 1)
+            pair_bank(q, 1, 0, "S")
+            for k in range(1, PAIR_BANKS):
+                pair_bank(q, 1, k, "V")
+            store(nc.sync, q * CHUNK_B + PAIR_B)
+
+        q = CHUNKS - 1
+        for a in range(PASSES):
+            for k in range(PAIR_BANKS):
+                pair_bank(q, a, k, "VS"[k % 2])
+                if (a, k) == (0, 1):
+                    store(nc.scalar, q * CHUNK_B - 1)
+            store(nc.sync, q * CHUNK_B + a * PAIR_B)
+            store(nc.scalar, q * CHUNK_B + a * PAIR_B + 1)

import concourse.mybir as mybir
from concourse.masks import make_identity

F32 = mybir.dt.float32
BF16 = mybir.dt.bfloat16
U32 = mybir.dt.uint32
U8 = mybir.dt.uint8
FP8X4 = mybir.dt.float8_e4m3fn_x4

P = 128
PACK = 4
PAIRS = PACK // 2
K_PASS = P * PACK

NODES = 1024
BATCH = 16
D_IN = 8
D_STATE = 64
D_CAND = D_IN + D_STATE
MATS = 2

PASSES = NODES // K_PASS
ROW_TILES = NODES // P
LOAD_TILES = 2
HALVES = 2
HALF_TILES = ROW_TILES // HALVES
HALF_ROWS = HALF_TILES * MATS
X_COLS = BATCH * D_IN
CHUNK_B = 4
CHUNKS = BATCH // CHUNK_B
CHUNK_COLS = CHUNK_B * D_STATE
PAIR_B = 2
PAIR_COLS = PAIR_B * D_STATE
BANK_F32 = 512
X_GROUPS = BANK_F32 // X_COLS
PAIR_ROWS = BANK_F32 // PAIR_COLS
PAIR_BANKS = ROW_TILES * MATS // PAIR_ROWS
PSUM_BANKS = 8

FLOPS = 2 * MATS * NODES * NODES * BATCH * D_CAND


def tile_agcrnlayer_pb_kernel(tc, adj, cheb2, x, state, r_logit, out):
    nc = tc.nc

    with tc.tile_pool(name="keep", bufs=1) as keep, tc.tile_pool(
        name="stage", bufs=2
    ) as stage, tc.tile_pool(name="flip", bufs=4) as flip, tc.psum_pool(
        name="psum", bufs=PSUM_BANKS
    ) as psum, tc.manual_schedule():
        ident = keep.tile([P, P], F32)
        mat_sb = [
            keep.tile([P, ROW_TILES, NODES], BF16, name="mat_sb%d" % s) for s in range(MATS)
        ]
        a_codes = keep.tile([P, MATS, ROW_TILES, PASSES, P], U32, align_bytes=64)
        a_scales = keep.tile([P, MATS, ROW_TILES, PASSES, P], U8, align_bytes=64)

        x_rows = keep.tile([P, BATCH, PASSES * PACK * D_IN], BF16)
        spread = keep.tile([P, PASSES, PASSES, P], BF16)
        x_grouped = keep.tile([P, PASSES, BATCH, D_IN, PACK], BF16, align_bytes=64)
        x_codes = keep.tile([P, PASSES, X_COLS], U32, align_bytes=64)
        x_scales = keep.tile([P, PASSES, X_COLS], U8, align_bytes=64)

        raw_shape = [P, PASSES, CHUNK_B, PACK * D_STATE]
        logit_raw = [keep.tile(raw_shape, BF16, name="logit_raw%d" % q) for q in range(CHUNKS)]
        state_raw = [keep.tile(raw_shape, BF16, name="state_raw%d" % q) for q in range(CHUNKS)]
        c_codes = [
            keep.tile([P, PASSES, CHUNK_COLS], U32, name="c_codes%d" % q, align_bytes=64)
            for q in range(CHUNKS)
        ]
        c_scales = [
            keep.tile([P, PASSES, CHUNK_COLS], U8, name="c_scales%d" % q, align_bytes=64)
            for q in range(CHUNKS)
        ]
        out_sb = keep.tile([P, BATCH, ROW_TILES * MATS, D_CAND], F32)
        gates = {}
        cands = {}
        waiting = []

        def load_pass(dst, src, g):
            k_rows = src[:, g * K_PASS : (g + 1) * K_PASS, :]
            nc.sync.dma_start(out=dst, in_=k_rows.rearrange("b (p t) c -> p b (t c)", t=PACK))

        def load_chunk(q):
            batches = slice(q * CHUNK_B, (q + 1) * CHUNK_B)
            for g in range(PASSES):
                load_pass(logit_raw[q][:, g], r_logit[batches], g)
                load_pass(state_raw[q][:, g], state[batches], g)

        def load_matrices(h):
            for j in range(h * HALF_TILES, (h + 1) * HALF_TILES, LOAD_TILES):
                for s, mat in enumerate((adj, cheb2)):
                    tiles = mat.rearrange("(p j) n -> p j n", j=ROW_TILES)
                    nc.sync.dma_start(
                        out=mat_sb[s][:, j : j + LOAD_TILES, :],
                        in_=tiles[:, j : j + LOAD_TILES, :],
                    )

        def words_side_by_side(raw):
            return raw.rearrange("p b (t c) -> p b c t", t=PACK)

        def gate_sigmoid(q, g):
            if g == 0:
                gates[q] = stage.tile([P, PASSES, CHUNK_B, PACK, D_STATE], F32, name="gate")
                cands[q] = stage.tile(
                    [P, PASSES, CHUNK_B, D_STATE, PACK], BF16, name="cand", align_bytes=64
                )
            nc.scalar.activation(
                out=gates[q][:, g].rearrange("p b t c -> p b (t c)"),
                in_=logit_raw[q][:, g],
                func=mybir.ActivationFunctionType.Sigmoid,
            )

        def gate_product(q, g):
            nc.vector.tensor_tensor(
                out=cands[q][:, g],
                in0=gates[q][:, g].rearrange("p b t c -> p b c t"),
                in1=words_side_by_side(state_raw[q][:, g]),
                op=mybir.AluOpType.mult,
            )

        def gate_quantise(q, g):
            nc.vector.quantize_mx(
                out=c_codes[q][:, g, :].bitcast(FP8X4),
                scales=c_scales[q][:, g, :],
                in_=cands[q][:, g].rearrange("p b c t -> p (b c t)"),
            )

        def copier(engine):
            return nc.vector.tensor_copy if engine == "V" else nc.scalar.copy

        def quantise_waiting():
            s, j, grouped = waiting.pop()
            nc.vector.quantize_mx(
                out=a_codes[:, s, j].rearrange("p g m -> p (g m)").bitcast(FP8X4),
                scales=a_scales[:, s, j].rearrange("p g m -> p (g m)"),
                in_=grouped[:].rearrange("p g m t -> p (g m t)"),
            )

        def transpose_tile(s, j, engine):
            words = mat_sb[s][:].bitcast(F32)
            flipped = psum.tile([P, PASSES, PAIRS, P], F32, tag="bank")
            for g in range(PASSES):
                for u in range(PAIRS):
                    first = g * P * PAIRS + u
                    nc.tensor.transpose(
                        flipped[:, g, u, :],
                        words[:, j, first : (g + 1) * P * PAIRS : PAIRS],
                        ident[:],
                    )
            grouped = flip.tile([P, PASSES, P, PACK], BF16, align_bytes=64)
            copier(engine)(
                out=grouped[:].bitcast(F32), in_=flipped[:].rearrange("p g u m -> p g m u")
            )
            if waiting:
                quantise_waiting()
            waiting.append((s, j, grouped))

        def multiply(acc, s, j, codes, scales):
            for g in range(PASSES):
                nc.tensor.matmul_mx(
                    out=acc,
                    lhsT=a_codes[:, s, j, g, :].bitcast(FP8X4),
                    lhsT_scale=a_scales[:, s, j, g, :],
                    rhs=codes[:, g, :].bitcast(FP8X4),
                    rhs_scale=scales[:, g, :],
                    start=(g == 0),
                    stop=(g == PASSES - 1),
                )

        def pair_bank(q, a, k, engine):
            first_b = q * CHUNK_B + a * PAIR_B
            cols = slice(a * PAIR_COLS, (a + 1) * PAIR_COLS)
            rows = slice(k * PAIR_ROWS, (k + 1) * PAIR_ROWS)
            acc = psum.tile([P, PAIR_ROWS, PAIR_COLS], F32, tag="bank")
            for i in range(PAIR_ROWS):
                row = k * PAIR_ROWS + i
                multiply(
                    acc[:, i, :],
                    row % MATS,
                    row // MATS,
                    c_codes[q][:, :, cols],
                    c_scales[q][:, :, cols],
                )
            copier(engine)(
                out=out_sb[:, first_b : first_b + PAIR_B, rows, D_IN:D_CAND].rearrange(
                    "p b r c -> p r b c"
                ),
                in_=acc[:].rearrange("p r (b c) -> p r b c", c=D_STATE),
            )

        def x_words(g, engine):
            moved = psum.tile([P, BATCH, PACK * D_IN], F32, tag="bank")
            for e in range(PASSES):
                nc.tensor.matmul(
                    moved[:],
                    lhsT=spread[:, g, e, :],
                    rhs=x_rows[:, :, e * PACK * D_IN : (e + 1) * PACK * D_IN],
                    start=(e == 0),
                    stop=(e == PASSES - 1),
                )
            copier(engine)(out=x_grouped[:, g], in_=words_side_by_side(moved[:]))

        def x_quantise():
            nc.vector.quantize_mx(
                out=x_codes[:].rearrange("p g w -> p (g w)").bitcast(FP8X4),
                scales=x_scales[:].rearrange("p g w -> p (g w)"),
                in_=x_grouped[:].rearrange("p g b c t -> p (g b c t)"),
            )

        def x_bank(k, engine):
            first_row = k * X_GROUPS
            acc = psum.tile([P, X_GROUPS, X_COLS], F32, tag="bank")
            for i in range(X_GROUPS):
                row = first_row + i
                multiply(acc[:, i, :], row % MATS, row // MATS, x_codes, x_scales)
            copier(engine)(
                out=out_sb[:, :, first_row : first_row + X_GROUPS, 0:D_IN].rearrange(
                    "p b r c -> p r b c"
                ),
                in_=acc[:].rearrange("p r (b c) -> p r b c", c=D_IN),
            )

        def store(queue, b):
            queue.dma_start(
                out=out[b].rearrange("(p j) s c -> p (j s c)", j=ROW_TILES),
                in_=out_sb[:, b].rearrange("p r c -> p (r c)"),
            )

        make_identity(nc, ident[:])
        nc.gpsimd.memset(spread[:], 0.0)
        for g in range(PASSES):
            for e in range(PASSES):
                nc.gpsimd.tensor_copy(
                    out=spread[:, g, e, e:P:PASSES],
                    in_=ident[:, g * (P // PASSES) : (g + 1) * (P // PASSES)],
                )

        load_chunk(0)
        load_matrices(0)
        load_matrices(1)
        nc.sync.dma_start(
            out=x_rows[:], in_=x.rearrange("b (q r) c -> q b (r c)", r=PASSES * PACK)
        )
        load_chunk(1)
        load_chunk(2)
        load_chunk(3)

        for g in range(PASSES):
            gate_sigmoid(0, g)
            gate_product(0, g)
        for g in range(PASSES):
            gate_quantise(0, g)

        for j in range(0, ROW_TILES, LOAD_TILES):
            for s in range(MATS):
                for k in range(LOAD_TILES):
                    last_of_load = (s, k) == (MATS - 1, LOAD_TILES - 1)
                    if last_of_load and j == ROW_TILES - LOAD_TILES:
                        gate_sigmoid(1, 0)
                    transpose_tile(s, j + k, "V" if last_of_load and j > 0 else "S")
            quantise_waiting()

        x_words(0, "S")
        gate_sigmoid(1, 1)
        x_words(1, "V")
        x_quantise()

        for k in range(PAIR_BANKS):
            if k == PAIR_BANKS - 1:
                gate_product(1, 0)
            pair_bank(0, 0, k, "S")
        gate_product(1, 1)
        x_bank(0, "V")
        x_bank(1, "S")
        x_bank(2, "S")
        gate_quantise(1, 0)
        x_bank(3, "V")
        store(nc.sync, 0)
        gate_sigmoid(2, 0)
        gate_quantise(1, 1)
        pair_bank(0, 1, 0, "S")
        store(nc.scalar, 1)
        for k in range(1, PAIR_BANKS):
            pair_bank(0, 1, k, "V")
        store(nc.sync, 2)

        for q in range(1, CHUNKS - 1):
            gate_sigmoid(q + 1, 1)
            pair_bank(q, 0, 0, "S")
            store(nc.scalar, q * CHUNK_B - 1)
            gate_product(q + 1, 0)
            pair_bank(q, 0, 1, "S")
            gate_product(q + 1, 1)
            pair_bank(q, 0, 2, "S")
            gate_quantise(q + 1, 0)
            pair_bank(q, 0, 3, "S")
            store(nc.sync, q * CHUNK_B)
            store(nc.scalar, q * CHUNK_B + 1)
            if q + 2 < CHUNKS:
                gate_sigmoid(q + 2, 0)
            gate_quantise(q + 1, 1)
            pair_bank(q, 1, 0, "S")
            for k in range(1, PAIR_BANKS):
                pair_bank(q, 1, k, "V")
            store(nc.sync, q * CHUNK_B + PAIR_B)

        q = CHUNKS - 1
        for a in range(PASSES):
            for k in range(PAIR_BANKS):
                pair_bank(q, a, k, "VS"[k % 2])
                if (a, k) == (0, 1):
                    store(nc.scalar, q * CHUNK_B - 1)
            store(nc.sync, q * CHUNK_B + a * PAIR_B)
            store(nc.scalar, q * CHUNK_B + a * PAIR_B + 1)
